import numpy as np
import ml_dtypes

BF16 = ml_dtypes.bfloat16


def bf(x):
    return np.asarray(x, np.float32).astype(BF16)


def f32(x):
    return np.asarray(x, np.float32)


def f64(x):
    return np.asarray(x).astype(np.float64)


def striped(idx):
    return np.tile(idx.reshape(-1, 16).T, (8, 1))


D, S, N = 128, 1024, 512
QGAIN = 2.0


def setup_inputs():
    return {"x": bf(np.random.standard_normal((D, S))), "wq": bf(QGAIN * np.random.standard_normal((D, D)) / np.sqrt(D)), "bq": f32(0.1 * np.random.standard_normal((D, 1))), "offs": striped(np.random.permutation(S)[:N])}


def reference(x, wq, bq, offs):
    idx = offs[:16].T.reshape(-1)
    xs = f64(x)
    q = f64(wq).T @ xs[:, idx] + f64(bq)
    scores = xs.T @ q / np.sqrt(D)
    e = np.exp(scores - scores.max(axis=0, keepdims=True))
    attn = e / e.sum(axis=0, keepdims=True)
    return xs @ attn

@@ -1,0 +1,117 @@
+import math
+
+import concourse.mybir as mybir
+from concourse.masks import make_identity
+
+BF16, F32, U16 = mybir.dt.bfloat16, mybir.dt.float32, mybir.dt.uint16
+EXP = mybir.ActivationFunctionType.Exp
+AX_X = mybir.AxisListType.X
+ALU = mybir.AluOpType
+
+P = 128
+D = 128
+S = 1024
+N = 512
+BANK = 512
+S_BLOCKS = S // P
+S_HALVES = S // BANK
+Q_BLOCKS = N // P
+SCALE = 1.0 / math.sqrt(D)
+
+FLOPS = 2 * D * N * (D + S + S)
+
+
+def tile_scatteringawareattention_kernel(tc, x, wq, bq, offs, out):
+    nc = tc.nc
+    with (
+        tc.tile_pool(name="held", bufs=1) as held,
+        tc.tile_pool(name="work", bufs=2) as work,
+        tc.tile_pool(name="stats", bufs=4) as stats,
+        tc.psum_pool(name="psum_scores", bufs=4) as psum_scores,
+        tc.psum_pool(name="psum_flip", bufs=2) as psum_flip,
+        tc.psum_pool(name="psum_out", bufs=1) as psum_out,
+    ):
+        offsets = held.tile([P, N // 16], U16, name="offsets")
+        nc.sync.dma_start(offsets[:], offs)
+        x_sb = held.tile([D, S], BF16, name="x_sb")
+        nc.sync.dma_start(x_sb[:], x)
+        wq_sb = held.tile([D, D], BF16, name="wq_sb")
+        nc.scalar.dma_start(wq_sb[:], wq)
+        bq_sb = held.tile([D, 1], F32, name="bq_sb")
+        nc.scalar.dma_start(bq_sb[:], bq)
+
+        ident_bf = held.tile([P, P], BF16, name="ident_bf")
+        make_identity(nc, ident_bf[:])
+        ident_f32 = held.tile([P, P], F32, name="ident_f32")
+        make_identity(nc, ident_f32[:])
+
+        q_ps = psum_scores.tile([D, N], F32, name="q_ps", tag="bank")
+        nc.tensor.matmul(q_ps[:], wq_sb[:], x_sb[:].indirect(offsets[:]), start=True, stop=True)
+        q_bf = held.tile([D, N], BF16, name="q_bf")
+        nc.vector.tensor_scalar_add(q_bf[:], q_ps[:], bq_sb[:, 0:1])
+
+        xT_ps = psum_flip.tile([P, S_BLOCKS, D], BF16, name="xT_ps", tag="flip")
+        for sb in range(S_BLOCKS):
+            nc.tensor.transpose(xT_ps[:, sb, :], x_sb[:, sb * P : (sb + 1) * P], ident_bf[:])
+        xT = held.tile([P, S_BLOCKS, D], BF16, name="xT")
+        nc.scalar.copy(xT[:], xT_ps[:])
+
+        def weights_of(jb):
+            row_max = stats.tile([P, S_HALVES], F32, name="row_max")
+            score_ps = []
+            for h in range(S_HALVES):
+                bank = psum_scores.tile([P, BANK], F32, name="score_ps", tag="bank")
+                nc.tensor.matmul(
+                    bank[:],
+                    q_bf[:, jb * P : (jb + 1) * P],
+                    x_sb[:, h * BANK : (h + 1) * BANK],
+                    start=True,
+                    stop=True,
+                )
+                nc.vector.reduce_max(row_max[:, h : h + 1], bank[:], axis=AX_X)
+                score_ps.append(bank)
+            shift = stats.tile([P, 1], F32, name="shift")
+            nc.vector.tensor_scalar(
+                shift[:], row_max[:, 0:1], row_max[:, 1:2], -SCALE, op0=ALU.max, op1=ALU.mult
+            )
+            e = work.tile([P, S], BF16, name="e")
+            row_sum = stats.tile([P, S_HALVES], F32, name="row_sum")
+            for h in range(S_HALVES):
+                nc.scalar.activation(
+                    e[:, h * BANK : (h + 1) * BANK],
+                    score_ps[h][:],
+                    EXP,
+                    bias=shift[:, 0:1],
+                    scale=SCALE,
+                    accum_out=row_sum[:, h : h + 1],
+                )
+            return e, row_sum
+
+        def attend(jb, e, row_sum):
+            den = stats.tile([P, 1], F32, name="den")
+            nc.vector.tensor_add(den[:], row_sum[:, 0:1], row_sum[:, 1:2])
+            rden = stats.tile([P, 1], F32, name="rden")
+            nc.vector.reciprocal(rden[:], den[:])
+            eT_ps = psum_flip.tile([P, S_BLOCKS, P], BF16, name="eT_ps", tag="flip")
+            for sb in range(S_BLOCKS):
+                nc.tensor.transpose(eT_ps[:, sb, :], e[:, sb * P : (sb + 1) * P], ident_bf[:])
+            eT = work.tile([P, S_BLOCKS, P], BF16, name="eT")
+            nc.scalar.copy(eT[:], eT_ps[:])
+            oT_ps = psum_out.tile([P, D], F32, name="oT_ps")
+            for sb in range(S_BLOCKS):
+                nc.tensor.matmul(
+                    oT_ps[:], eT[:, sb, :], xT[:, sb, :], start=(sb == 0), stop=(sb == S_BLOCKS - 1)
+                )
+            oT = work.tile([P, D], F32, name="oT")
+            nc.vector.tensor_scalar_mul(oT[:], oT_ps[:], rden[:, 0:1])
+            o_ps = psum_out.tile([D, P], F32, name="o_ps")
+            nc.tensor.transpose(o_ps[:], oT[:], ident_f32[:])
+            o_sb = work.tile([D, P], F32, name="o_sb")
+            nc.scalar.copy(o_sb[:], o_ps[:])
+            nc.sync.dma_start(out[:, jb * P : (jb + 1) * P], o_sb[:])
+
+        pending = weights_of(0)
+        for jb in range(Q_BLOCKS):
+            following = weights_of(jb + 1) if jb + 1 < Q_BLOCKS else None
+            attend(jb, pending[0], pending[1])
+            pending = following

@@ -5,6 +5,7 @@ from concourse.masks import make_identity
 
 BF16, F32, U16 = mybir.dt.bfloat16, mybir.dt.float32, mybir.dt.uint16
 EXP = mybir.ActivationFunctionType.Exp
+COPY = mybir.ActivationFunctionType.Copy
 AX_X = mybir.AxisListType.X
 ALU = mybir.AluOpType
 
@@ -15,7 +16,10 @@ N = 512
 BANK = 512
 S_BLOCKS = S // P
 S_HALVES = S // BANK
+HALF_BLOCKS = S_BLOCKS // S_HALVES
 Q_BLOCKS = N // P
+XT_PITCH = 136
+WARM_UP = 16
 SCALE = 1.0 / math.sqrt(D)
 
 FLOPS = 2 * D * N * (D + S + S)
@@ -31,6 +35,12 @@ def tile_scatteringawareattention_kernel(tc, x, wq, bq, offs, out):
         tc.psum_pool(name="psum_flip", bufs=2) as psum_flip,
         tc.psum_pool(name="psum_out", bufs=1) as psum_out,
     ):
+        zeros = held.tile([P, P], BF16, name="zeros")
+        nc.gpsimd.memset(zeros[:], 0.0)
+        warm_ps = psum_out.tile([P, P], F32, name="warm_ps", tag="o_ps")
+        for i in range(WARM_UP):
+            nc.tensor.matmul(warm_ps[:], zeros[:], zeros[:], start=True, stop=True)
+
         offsets = held.tile([P, N // 16], U16, name="offsets")
         nc.sync.dma_start(offsets[:], offs)
         x_sb = held.tile([D, S], BF16, name="x_sb")
@@ -45,16 +55,19 @@ def tile_scatteringawareattention_kernel(tc, x, wq, bq, offs, out):
         ident_f32 = held.tile([P, P], F32, name="ident_f32")
         make_identity(nc, ident_f32[:])
 
-        q_ps = psum_scores.tile([D, N], F32, name="q_ps", tag="bank")
-        nc.tensor.matmul(q_ps[:], wq_sb[:], x_sb[:].indirect(offsets[:]), start=True, stop=True)
         q_bf = held.tile([D, N], BF16, name="q_bf")
-        nc.vector.tensor_scalar_add(q_bf[:], q_ps[:], bq_sb[:, 0:1])
+        for jb in range(Q_BLOCKS):
+            q_ps = psum_scores.tile([D, P], F32, name="q_ps", tag="bank")
+            piece = offsets[:, jb * (P // 16) : (jb + 1) * (P // 16)]
+            nc.tensor.matmul(q_ps[:], wq_sb[:], x_sb[:].indirect(piece), start=True, stop=True)
+            nc.vector.tensor_scalar_add(q_bf[:, jb * P : (jb + 1) * P], q_ps[:], bq_sb[:, 0:1])
 
+        xT = held.tile([P, S_BLOCKS, XT_PITCH], BF16, name="xT")
+        nc.gpsimd.memset(xT[:], 1.0)
         xT_ps = psum_flip.tile([P, S_BLOCKS, D], BF16, name="xT_ps", tag="flip")
         for sb in range(S_BLOCKS):
             nc.tensor.transpose(xT_ps[:, sb, :], x_sb[:, sb * P : (sb + 1) * P], ident_bf[:])
-        xT = held.tile([P, S_BLOCKS, D], BF16, name="xT")
-        nc.scalar.copy(xT[:], xT_ps[:])
+        nc.scalar.copy(xT[:, :, 0:D], xT_ps[:])
 
         def weights_of(jb):
             row_max = stats.tile([P, S_HALVES], F32, name="row_max")
@@ -75,7 +88,6 @@ def tile_scatteringawareattention_kernel(tc, x, wq, bq, offs, out):
                 shift[:], row_max[:, 0:1], row_max[:, 1:2], -SCALE, op0=ALU.max, op1=ALU.mult
             )
             e = work.tile([P, S], BF16, name="e")
-            row_sum = stats.tile([P, S_HALVES], F32, name="row_sum")
             for h in range(S_HALVES):
                 nc.scalar.activation(
                     e[:, h * BANK : (h + 1) * BANK],
@@ -83,27 +95,30 @@ def tile_scatteringawareattention_kernel(tc, x, wq, bq, offs, out):
                     EXP,
                     bias=shift[:, 0:1],
                     scale=SCALE,
-                    accum_out=row_sum[:, h : h + 1],
                 )
-            return e, row_sum
+            return e
 
-        def attend(jb, e, row_sum):
-            den = stats.tile([P, 1], F32, name="den")
-            nc.vector.tensor_add(den[:], row_sum[:, 0:1], row_sum[:, 1:2])
-            rden = stats.tile([P, 1], F32, name="rden")
-            nc.vector.reciprocal(rden[:], den[:])
-            eT_ps = psum_flip.tile([P, S_BLOCKS, P], BF16, name="eT_ps", tag="flip")
-            for sb in range(S_BLOCKS):
-                nc.tensor.transpose(eT_ps[:, sb, :], e[:, sb * P : (sb + 1) * P], ident_bf[:])
+        def attend(jb, e):
             eT = work.tile([P, S_BLOCKS, P], BF16, name="eT")
-            nc.scalar.copy(eT[:], eT_ps[:])
-            oT_ps = psum_out.tile([P, D], F32, name="oT_ps")
+            for h in range(S_HALVES):
+                eT_ps = psum_flip.tile([P, HALF_BLOCKS, P], BF16, name="eT_ps", tag="flip")
+                for k in range(HALF_BLOCKS):
+                    sb = h * HALF_BLOCKS + k
+                    nc.tensor.transpose(eT_ps[:, k, :], e[:, sb * P : (sb + 1) * P], ident_bf[:])
+                half = eT[:, h * HALF_BLOCKS : (h + 1) * HALF_BLOCKS, :]
+                if h == 0:
+                    nc.vector.tensor_copy(half, eT_ps[:])
+                else:
+                    nc.scalar.copy(half, eT_ps[:])
+            oT_ps = psum_out.tile([P, D + 1], F32, name="oT_ps")
             for sb in range(S_BLOCKS):
                 nc.tensor.matmul(
-                    oT_ps[:], eT[:, sb, :], xT[:, sb, :], start=(sb == 0), stop=(sb == S_BLOCKS - 1)
+                    oT_ps[:], eT[:, sb, :], xT[:, sb, 0 : D + 1], start=(sb == 0), stop=(sb == S_BLOCKS - 1)
                 )
+            rden = stats.tile([P, 1], F32, name="rden")
+            nc.vector.reciprocal(rden[:], oT_ps[:, D : D + 1])
             oT = work.tile([P, D], F32, name="oT")
-            nc.vector.tensor_scalar_mul(oT[:], oT_ps[:], rden[:, 0:1])
+            nc.vector.tensor_scalar_mul(oT[:], oT_ps[:, 0:D], rden[:, 0:1])
             o_ps = psum_out.tile([D, P], F32, name="o_ps")
             nc.tensor.transpose(o_ps[:], oT[:], ident_f32[:])
             o_sb = work.tile([D, P], F32, name="o_sb")
@@ -113,5 +128,5 @@ def tile_scatteringawareattention_kernel(tc, x, wq, bq, offs, out):
         pending = weights_of(0)
         for jb in range(Q_BLOCKS):
             following = weights_of(jb + 1) if jb + 1 < Q_BLOCKS else None
-            attend(jb, pending[0], pending[1])
+            attend(jb, pending)
             pending = following

@@ -66,7 +66,7 @@ def tile_scatteringawareattention_kernel(tc, x, wq, bq, offs, out):
         nc.gpsimd.memset(xT[:], 1.0)
         xT_ps = psum_flip.tile([P, S_BLOCKS, D], BF16, name="xT_ps", tag="flip")
         for sb in range(S_BLOCKS):
-            nc.tensor.transpose(xT_ps[:, sb, :], x_sb[:, sb * P : (sb + 1) * P], ident_bf[:])
+            nc.tensor.matmul(xT_ps[:, sb, :], x_sb[:, sb * P : (sb + 1) * P], ident_bf[:], start=True, stop=True)
         nc.scalar.copy(xT[:, :, 0:D], xT_ps[:])
 
         def weights_of(jb):
@@ -104,7 +104,7 @@ def tile_scatteringawareattention_kernel(tc, x, wq, bq, offs, out):
                 eT_ps = psum_flip.tile([P, HALF_BLOCKS, P], BF16, name="eT_ps", tag="flip")
                 for k in range(HALF_BLOCKS):
                     sb = h * HALF_BLOCKS + k
-                    nc.tensor.transpose(eT_ps[:, k, :], e[:, sb * P : (sb + 1) * P], ident_bf[:])
+                    nc.tensor.matmul(eT_ps[:, k, :], e[:, sb * P : (sb + 1) * P], ident_bf[:], start=True, stop=True)
                 half = eT[:, h * HALF_BLOCKS : (h + 1) * HALF_BLOCKS, :]
                 if h == 0:
                     nc.vector.tensor_copy(half, eT_ps[:])

@@ -31,7 +31,7 @@ def tile_scatteringawareattention_kernel(tc, x, wq, bq, offs, out):
         tc.tile_pool(name="held", bufs=1) as held,
         tc.tile_pool(name="work", bufs=2) as work,
         tc.tile_pool(name="stats", bufs=4) as stats,
-        tc.psum_pool(name="psum_scores", bufs=4) as psum_scores,
+        tc.psum_pool(name="psum_scores", bufs=3) as psum_scores,
         tc.psum_pool(name="psum_flip", bufs=2) as psum_flip,
         tc.psum_pool(name="psum_out", bufs=1) as psum_out,
     ):
@@ -66,12 +66,12 @@ def tile_scatteringawareattention_kernel(tc, x, wq, bq, offs, out):
         nc.gpsimd.memset(xT[:], 1.0)
         xT_ps = psum_flip.tile([P, S_BLOCKS, D], BF16, name="xT_ps", tag="flip")
         for sb in range(S_BLOCKS):
-            nc.tensor.matmul(xT_ps[:, sb, :], x_sb[:, sb * P : (sb + 1) * P], ident_bf[:], start=True, stop=True)
+            nc.tensor.transpose(xT_ps[:, sb, :], x_sb[:, sb * P : (sb + 1) * P], ident_bf[:])
         nc.scalar.copy(xT[:, :, 0:D], xT_ps[:])
 
         def weights_of(jb):
+            scaled = work.tile([P, S], F32, name="scaled", bufs=3)
             row_max = stats.tile([P, S_HALVES], F32, name="row_max")
-            score_ps = []
             for h in range(S_HALVES):
                 bank = psum_scores.tile([P, BANK], F32, name="score_ps", tag="bank")
                 nc.tensor.matmul(
@@ -81,20 +81,26 @@ def tile_scatteringawareattention_kernel(tc, x, wq, bq, offs, out):
                     start=True,
                     stop=True,
                 )
-                nc.vector.reduce_max(row_max[:, h : h + 1], bank[:], axis=AX_X)
-                score_ps.append(bank)
+                nc.vector.tensor_scalar(
+                    scaled[:, h * BANK : (h + 1) * BANK],
+                    bank[:],
+                    SCALE,
+                    None,
+                    op0=ALU.mult,
+                    op1=ALU.max,
+                    accum_out=row_max[:, h : h + 1],
+                )
             shift = stats.tile([P, 1], F32, name="shift")
             nc.vector.tensor_scalar(
-                shift[:], row_max[:, 0:1], row_max[:, 1:2], -SCALE, op0=ALU.max, op1=ALU.mult
+                shift[:], row_max[:, 0:1], row_max[:, 1:2], -1.0, op0=ALU.max, op1=ALU.mult
             )
             e = work.tile([P, S], BF16, name="e")
             for h in range(S_HALVES):
                 nc.scalar.activation(
                     e[:, h * BANK : (h + 1) * BANK],
-                    score_ps[h][:],
+                    scaled[:, h * BANK : (h + 1) * BANK],
                     EXP,
                     bias=shift[:, 0:1],
-                    scale=SCALE,
                 )
             return e
 
@@ -104,13 +110,13 @@ def tile_scatteringawareattention_kernel(tc, x, wq, bq, offs, out):
                 eT_ps = psum_flip.tile([P, HALF_BLOCKS, P], BF16, name="eT_ps", tag="flip")
                 for k in range(HALF_BLOCKS):
                     sb = h * HALF_BLOCKS + k
-                    nc.tensor.matmul(eT_ps[:, k, :], e[:, sb * P : (sb + 1) * P], ident_bf[:], start=True, stop=True)
+                    nc.tensor.transpose(eT_ps[:, k, :], e[:, sb * P : (sb + 1) * P], ident_bf[:])
                 half = eT[:, h * HALF_BLOCKS : (h + 1) * HALF_BLOCKS, :]
                 if h == 0:
                     nc.vector.tensor_copy(half, eT_ps[:])
                 else:
                     nc.scalar.copy(half, eT_ps[:])
-            oT_ps = psum_out.tile([P, D + 1], F32, name="oT_ps")
+            oT_ps = psum_out.tile([P, D + 1], F32, name="oT_ps", bufs=2)
             for sb in range(S_BLOCKS):
                 nc.tensor.matmul(
                     oT_ps[:], eT[:, sb, :], xT[:, sb, 0 : D + 1], start=(sb == 0), stop=(sb == S_BLOCKS - 1)

@@ -18,7 +18,6 @@ S_BLOCKS = S // P
 S_HALVES = S // BANK
 HALF_BLOCKS = S_BLOCKS // S_HALVES
 Q_BLOCKS = N // P
-XT_PITCH = 136
 WARM_UP = 16
 SCALE = 1.0 / math.sqrt(D)
 
@@ -31,7 +30,7 @@ def tile_scatteringawareattention_kernel(tc, x, wq, bq, offs, out):
         tc.tile_pool(name="held", bufs=1) as held,
         tc.tile_pool(name="work", bufs=2) as work,
         tc.tile_pool(name="stats", bufs=4) as stats,
-        tc.psum_pool(name="psum_scores", bufs=3) as psum_scores,
+        tc.psum_pool(name="psum_scores", bufs=4) as psum_scores,
         tc.psum_pool(name="psum_flip", bufs=2) as psum_flip,
         tc.psum_pool(name="psum_out", bufs=1) as psum_out,
     ):
@@ -54,6 +53,8 @@ def tile_scatteringawareattention_kernel(tc, x, wq, bq, offs, out):
         make_identity(nc, ident_bf[:])
         ident_f32 = held.tile([P, P], F32, name="ident_f32")
         make_identity(nc, ident_f32[:])
+        ones_f32 = held.tile([P, P], F32, name="ones_f32")
+        nc.gpsimd.memset(ones_f32[:], 1.0)
 
         q_bf = held.tile([D, N], BF16, name="q_bf")
         for jb in range(Q_BLOCKS):
@@ -62,16 +63,15 @@ def tile_scatteringawareattention_kernel(tc, x, wq, bq, offs, out):
             nc.tensor.matmul(q_ps[:], wq_sb[:], x_sb[:].indirect(piece), start=True, stop=True)
             nc.vector.tensor_scalar_add(q_bf[:, jb * P : (jb + 1) * P], q_ps[:], bq_sb[:, 0:1])
 
-        xT = held.tile([P, S_BLOCKS, XT_PITCH], BF16, name="xT")
-        nc.gpsimd.memset(xT[:], 1.0)
+        xT = held.tile([P, S_BLOCKS, D], BF16, name="xT")
         xT_ps = psum_flip.tile([P, S_BLOCKS, D], BF16, name="xT_ps", tag="flip")
         for sb in range(S_BLOCKS):
             nc.tensor.transpose(xT_ps[:, sb, :], x_sb[:, sb * P : (sb + 1) * P], ident_bf[:])
-        nc.scalar.copy(xT[:, :, 0:D], xT_ps[:])
+        nc.scalar.copy(xT[:], xT_ps[:])
 
         def weights_of(jb):
-            scaled = work.tile([P, S], F32, name="scaled", bufs=3)
             row_max = stats.tile([P, S_HALVES], F32, name="row_max")
+            score_ps = []
             for h in range(S_HALVES):
                 bank = psum_scores.tile([P, BANK], F32, name="score_ps", tag="bank")
                 nc.tensor.matmul(
@@ -81,30 +81,32 @@ def tile_scatteringawareattention_kernel(tc, x, wq, bq, offs, out):
                     start=True,
                     stop=True,
                 )
-                nc.vector.tensor_scalar(
-                    scaled[:, h * BANK : (h + 1) * BANK],
-                    bank[:],
-                    SCALE,
-                    None,
-                    op0=ALU.mult,
-                    op1=ALU.max,
-                    accum_out=row_max[:, h : h + 1],
-                )
+                nc.vector.reduce_max(row_max[:, h : h + 1], bank[:], axis=AX_X)
+                score_ps.append(bank)
             shift = stats.tile([P, 1], F32, name="shift")
             nc.vector.tensor_scalar(
-                shift[:], row_max[:, 0:1], row_max[:, 1:2], -1.0, op0=ALU.max, op1=ALU.mult
+                shift[:], row_max[:, 0:1], row_max[:, 1:2], -SCALE, op0=ALU.max, op1=ALU.mult
             )
             e = work.tile([P, S], BF16, name="e")
+            row_sum = stats.tile([P, S_HALVES], F32, name="row_sum")
             for h in range(S_HALVES):
                 nc.scalar.activation(
                     e[:, h * BANK : (h + 1) * BANK],
-                    scaled[:, h * BANK : (h + 1) * BANK],
+                    score_ps[h][:],
                     EXP,
                     bias=shift[:, 0:1],
+                    scale=SCALE,
+                    accum_out=row_sum[:, h : h + 1],
                 )
-            return e
+            return e, row_sum
 
-        def attend(jb, e):
+        def attend(jb, e, row_sum):
+            den = stats.tile([P, 1], F32, name="den")
+            nc.vector.tensor_add(den[:], row_sum[:, 0:1], row_sum[:, 1:2])
+            rden = stats.tile([P, 1], F32, name="rden")
+            nc.vector.reciprocal(rden[:], den[:])
+            diag = work.tile([P, P], F32, name="diag")
+            nc.vector.tensor_scalar_mul(diag[:], ident_f32[:], rden[:, 0:1])
             eT = work.tile([P, S_BLOCKS, P], BF16, name="eT")
             for h in range(S_HALVES):
                 eT_ps = psum_flip.tile([P, HALF_BLOCKS, P], BF16, name="eT_ps", tag="flip")
@@ -116,23 +118,21 @@ def tile_scatteringawareattention_kernel(tc, x, wq, bq, offs, out):
                     nc.vector.tensor_copy(half, eT_ps[:])
                 else:
                     nc.scalar.copy(half, eT_ps[:])
-            oT_ps = psum_out.tile([P, D + 1], F32, name="oT_ps", bufs=2)
+            spread_ps = psum_out.tile([D, P], F32, name="spread_ps")
+            nc.tensor.matmul(spread_ps[:], ones_f32[:], diag[:], start=True, stop=True)
+            spread = work.tile([D, P], F32, name="spread")
+            nc.scalar.copy(spread[:], spread_ps[:])
+            o_ps = psum_out.tile([D, P], F32, name="o_ps")
             for sb in range(S_BLOCKS):
                 nc.tensor.matmul(
-                    oT_ps[:], eT[:, sb, :], xT[:, sb, 0 : D + 1], start=(sb == 0), stop=(sb == S_BLOCKS - 1)
+                    o_ps[:], xT[:, sb, :], eT[:, sb, :], start=(sb == 0), stop=(sb == S_BLOCKS - 1)
                 )
-            rden = stats.tile([P, 1], F32, name="rden")
-            nc.vector.reciprocal(rden[:], oT_ps[:, D : D + 1])
-            oT = work.tile([P, D], F32, name="oT")
-            nc.vector.tensor_scalar_mul(oT[:], oT_ps[:, 0:D], rden[:, 0:1])
-            o_ps = psum_out.tile([D, P], F32, name="o_ps")
-            nc.tensor.transpose(o_ps[:], oT[:], ident_f32[:])
             o_sb = work.tile([D, P], F32, name="o_sb")
-            nc.scalar.copy(o_sb[:], o_ps[:])
+            nc.vector.tensor_mul(o_sb[:], o_ps[:], spread[:])
             nc.sync.dma_start(out[:, jb * P : (jb + 1) * P], o_sb[:])
 
         pending = weights_of(0)
         for jb in range(Q_BLOCKS):
             following = weights_of(jb + 1) if jb + 1 < Q_BLOCKS else None
-            attend(jb, pending)
+            attend(jb, pending[0], pending[1])
             pending = following

@@ -57,17 +57,12 @@ def tile_scatteringawareattention_kernel(tc, x, wq, bq, offs, out):
         nc.gpsimd.memset(ones_f32[:], 1.0)
 
         q_bf = held.tile([D, N], BF16, name="q_bf")
-        for jb in range(Q_BLOCKS):
+
+        def project(jb):
             q_ps = psum_scores.tile([D, P], F32, name="q_ps", tag="bank")
             piece = offsets[:, jb * (P // 16) : (jb + 1) * (P // 16)]
             nc.tensor.matmul(q_ps[:], wq_sb[:], x_sb[:].indirect(piece), start=True, stop=True)
             nc.vector.tensor_scalar_add(q_bf[:, jb * P : (jb + 1) * P], q_ps[:], bq_sb[:, 0:1])
-
-        xT = held.tile([P, S_BLOCKS, D], BF16, name="xT")
-        xT_ps = psum_flip.tile([P, S_BLOCKS, D], BF16, name="xT_ps", tag="flip")
-        for sb in range(S_BLOCKS):
-            nc.tensor.transpose(xT_ps[:, sb, :], x_sb[:, sb * P : (sb + 1) * P], ident_bf[:])
-        nc.scalar.copy(xT[:], xT_ps[:])
 
         def weights_of(jb):
             row_max = stats.tile([P, S_HALVES], F32, name="row_max")
@@ -121,7 +116,7 @@ def tile_scatteringawareattention_kernel(tc, x, wq, bq, offs, out):
             spread_ps = psum_out.tile([D, P], F32, name="spread_ps")
             nc.tensor.matmul(spread_ps[:], ones_f32[:], diag[:], start=True, stop=True)
             spread = work.tile([D, P], F32, name="spread")
-            nc.scalar.copy(spread[:], spread_ps[:])
+            nc.vector.tensor_copy(spread[:], spread_ps[:])
             o_ps = psum_out.tile([D, P], F32, name="o_ps")
             for sb in range(S_BLOCKS):
                 nc.tensor.matmul(
@@ -131,7 +126,18 @@ def tile_scatteringawareattention_kernel(tc, x, wq, bq, offs, out):
             nc.vector.tensor_mul(o_sb[:], o_ps[:], spread[:])
             nc.sync.dma_start(out[:, jb * P : (jb + 1) * P], o_sb[:])
 
+        for jb in range(Q_BLOCKS):
+            project(jb)
         pending = weights_of(0)
+
+        xT = held.tile([P, S_BLOCKS, D], BF16, name="xT")
+        for h in range(S_HALVES):
+            xT_ps = psum_flip.tile([P, HALF_BLOCKS, D], BF16, name="xT_ps", tag="flip")
+            for k in range(HALF_BLOCKS):
+                sb = h * HALF_BLOCKS + k
+                nc.tensor.transpose(xT_ps[:, k, :], x_sb[:, sb * P : (sb + 1) * P], ident_bf[:])
+            nc.scalar.copy(xT[:, h * HALF_BLOCKS : (h + 1) * HALF_BLOCKS, :], xT_ps[:])
+
         for jb in range(Q_BLOCKS):
             following = weights_of(jb + 1) if jb + 1 < Q_BLOCKS else None
             attend(jb, pending[0], pending[1])

@@ -18,7 +18,6 @@ S_BLOCKS = S // P
 S_HALVES = S // BANK
 HALF_BLOCKS = S_BLOCKS // S_HALVES
 Q_BLOCKS = N // P
-WARM_UP = 16
 SCALE = 1.0 / math.sqrt(D)
 
 FLOPS = 2 * D * N * (D + S + S)
@@ -34,12 +33,6 @@ def tile_scatteringawareattention_kernel(tc, x, wq, bq, offs, out):
         tc.psum_pool(name="psum_flip", bufs=2) as psum_flip,
         tc.psum_pool(name="psum_out", bufs=1) as psum_out,
     ):
-        zeros = held.tile([P, P], BF16, name="zeros")
-        nc.gpsimd.memset(zeros[:], 0.0)
-        warm_ps = psum_out.tile([P, P], F32, name="warm_ps", tag="o_ps")
-        for i in range(WARM_UP):
-            nc.tensor.matmul(warm_ps[:], zeros[:], zeros[:], start=True, stop=True)
-
         offsets = held.tile([P, N // 16], U16, name="offsets")
         nc.sync.dma_start(offsets[:], offs)
         x_sb = held.tile([D, S], BF16, name="x_sb")
@@ -57,12 +50,17 @@ def tile_scatteringawareattention_kernel(tc, x, wq, bq, offs, out):
         nc.gpsimd.memset(ones_f32[:], 1.0)
 
         q_bf = held.tile([D, N], BF16, name="q_bf")
-
-        def project(jb):
+        for jb in range(Q_BLOCKS):
             q_ps = psum_scores.tile([D, P], F32, name="q_ps", tag="bank")
             piece = offsets[:, jb * (P // 16) : (jb + 1) * (P // 16)]
             nc.tensor.matmul(q_ps[:], wq_sb[:], x_sb[:].indirect(piece), start=True, stop=True)
             nc.vector.tensor_scalar_add(q_bf[:, jb * P : (jb + 1) * P], q_ps[:], bq_sb[:, 0:1])
+
+        xT = held.tile([P, S_BLOCKS, D], BF16, name="xT")
+        xT_ps = psum_flip.tile([P, S_BLOCKS, D], BF16, name="xT_ps", tag="flip")
+        for sb in range(S_BLOCKS):
+            nc.tensor.transpose(xT_ps[:, sb, :], x_sb[:, sb * P : (sb + 1) * P], ident_bf[:])
+        nc.scalar.copy(xT[:], xT_ps[:])
 
         def weights_of(jb):
             row_max = stats.tile([P, S_HALVES], F32, name="row_max")
@@ -126,18 +124,7 @@ def tile_scatteringawareattention_kernel(tc, x, wq, bq, offs, out):
             nc.vector.tensor_mul(o_sb[:], o_ps[:], spread[:])
             nc.sync.dma_start(out[:, jb * P : (jb + 1) * P], o_sb[:])
 
-        for jb in range(Q_BLOCKS):
-            project(jb)
         pending = weights_of(0)
-
-        xT = held.tile([P, S_BLOCKS, D], BF16, name="xT")
-        for h in range(S_HALVES):
-            xT_ps = psum_flip.tile([P, HALF_BLOCKS, D], BF16, name="xT_ps", tag="flip")
-            for k in range(HALF_BLOCKS):
-                sb = h * HALF_BLOCKS + k
-                nc.tensor.transpose(xT_ps[:, k, :], x_sb[:, sb * P : (sb + 1) * P], ident_bf[:])
-            nc.scalar.copy(xT[:, h * HALF_BLOCKS : (h + 1) * HALF_BLOCKS, :], xT_ps[:])
-
         for jb in range(Q_BLOCKS):
             following = weights_of(jb + 1) if jb + 1 < Q_BLOCKS else None
             attend(jb, pending[0], pending[1])

@@ -18,6 +18,7 @@ S_BLOCKS = S // P
 S_HALVES = S // BANK
 HALF_BLOCKS = S_BLOCKS // S_HALVES
 Q_BLOCKS = N // P
+WARM_UP = 16
 SCALE = 1.0 / math.sqrt(D)
 
 FLOPS = 2 * D * N * (D + S + S)
@@ -33,6 +34,12 @@ def tile_scatteringawareattention_kernel(tc, x, wq, bq, offs, out):
         tc.psum_pool(name="psum_flip", bufs=2) as psum_flip,
         tc.psum_pool(name="psum_out", bufs=1) as psum_out,
     ):
+        zeros = held.tile([P, P], BF16, name="zeros")
+        nc.gpsimd.memset(zeros[:], 0.0)
+        warm_ps = psum_out.tile([P, P], F32, name="warm_ps", tag="o_ps")
+        for i in range(WARM_UP):
+            nc.tensor.matmul(warm_ps[:], zeros[:], zeros[:], start=True, stop=True)
+
         offsets = held.tile([P, N // 16], U16, name="offsets")
         nc.sync.dma_start(offsets[:], offs)
         x_sb = held.tile([D, S], BF16, name="x_sb")

@@ -5,8 +5,6 @@ from concourse.masks import make_identity
 
 BF16, F32, U16 = mybir.dt.bfloat16, mybir.dt.float32, mybir.dt.uint16
 EXP = mybir.ActivationFunctionType.Exp
-COPY = mybir.ActivationFunctionType.Copy
-AX_X = mybir.AxisListType.X
 ALU = mybir.AluOpType
 
 P = 128
@@ -28,10 +26,10 @@ def tile_scatteringawareattention_kernel(tc, x, wq, bq, offs, out):
     nc = tc.nc
     with (
         tc.tile_pool(name="held", bufs=1) as held,
-        tc.tile_pool(name="work", bufs=2) as work,
+        tc.tile_pool(name="work", bufs=3) as work,
         tc.tile_pool(name="stats", bufs=4) as stats,
-        tc.psum_pool(name="psum_scores", bufs=4) as psum_scores,
-        tc.psum_pool(name="psum_flip", bufs=2) as psum_flip,
+        tc.psum_pool(name="psum_scores", bufs=3) as psum_scores,
+        tc.psum_pool(name="psum_flip", bufs=3) as psum_flip,
         tc.psum_pool(name="psum_out", bufs=1) as psum_out,
     ):
         zeros = held.tile([P, P], BF16, name="zeros")
@@ -53,8 +51,6 @@ def tile_scatteringawareattention_kernel(tc, x, wq, bq, offs, out):
         make_identity(nc, ident_bf[:])
         ident_f32 = held.tile([P, P], F32, name="ident_f32")
         make_identity(nc, ident_f32[:])
-        ones_f32 = held.tile([P, P], F32, name="ones_f32")
-        nc.gpsimd.memset(ones_f32[:], 1.0)
 
         q_bf = held.tile([D, N], BF16, name="q_bf")
         for jb in range(Q_BLOCKS):
@@ -67,11 +63,11 @@ def tile_scatteringawareattention_kernel(tc, x, wq, bq, offs, out):
         xT_ps = psum_flip.tile([P, S_BLOCKS, D], BF16, name="xT_ps", tag="flip")
         for sb in range(S_BLOCKS):
             nc.tensor.transpose(xT_ps[:, sb, :], x_sb[:, sb * P : (sb + 1) * P], ident_bf[:])
-        nc.scalar.copy(xT[:], xT_ps[:])
+        nc.vector.tensor_copy(xT[:], xT_ps[:])
 
-        def weights_of(jb):
-            row_max = stats.tile([P, S_HALVES], F32, name="row_max")
-            score_ps = []
+        def scores_of(jb):
+            negated = work.tile([P, S], F32, name="negated")
+            lowest = stats.tile([P, S_HALVES], F32, name="lowest")
             for h in range(S_HALVES):
                 bank = psum_scores.tile([P, BANK], F32, name="score_ps", tag="bank")
                 nc.tensor.matmul(
@@ -81,21 +77,27 @@ def tile_scatteringawareattention_kernel(tc, x, wq, bq, offs, out):
                     start=True,
                     stop=True,
                 )
-                nc.vector.reduce_max(row_max[:, h : h + 1], bank[:], axis=AX_X)
-                score_ps.append(bank)
-            shift = stats.tile([P, 1], F32, name="shift")
-            nc.vector.tensor_scalar(
-                shift[:], row_max[:, 0:1], row_max[:, 1:2], -SCALE, op0=ALU.max, op1=ALU.mult
-            )
+                nc.vector.tensor_scalar(
+                    negated[:, h * BANK : (h + 1) * BANK],
+                    bank[:],
+                    -SCALE,
+                    None if h == 0 else lowest[:, h - 1 : h],
+                    op0=ALU.mult,
+                    op1=ALU.min,
+                    accum_out=lowest[:, h : h + 1],
+                )
+            return negated, lowest[:, S_HALVES - 1 : S_HALVES]
+
+        def weights_of(negated, shift):
             e = work.tile([P, S], BF16, name="e")
             row_sum = stats.tile([P, S_HALVES], F32, name="row_sum")
             for h in range(S_HALVES):
                 nc.scalar.activation(
                     e[:, h * BANK : (h + 1) * BANK],
-                    score_ps[h][:],
+                    negated[:, h * BANK : (h + 1) * BANK],
                     EXP,
-                    bias=shift[:, 0:1],
-                    scale=SCALE,
+                    bias=shift,
+                    scale=-1.0,
                     accum_out=row_sum[:, h : h + 1],
                 )
             return e, row_sum
@@ -105,8 +107,6 @@ def tile_scatteringawareattention_kernel(tc, x, wq, bq, offs, out):
             nc.vector.tensor_add(den[:], row_sum[:, 0:1], row_sum[:, 1:2])
             rden = stats.tile([P, 1], F32, name="rden")
             nc.vector.reciprocal(rden[:], den[:])
-            diag = work.tile([P, P], F32, name="diag")
-            nc.vector.tensor_scalar_mul(diag[:], ident_f32[:], rden[:, 0:1])
             eT = work.tile([P, S_BLOCKS, P], BF16, name="eT")
             for h in range(S_HALVES):
                 eT_ps = psum_flip.tile([P, HALF_BLOCKS, P], BF16, name="eT_ps", tag="flip")
@@ -114,12 +114,9 @@ def tile_scatteringawareattention_kernel(tc, x, wq, bq, offs, out):
                     sb = h * HALF_BLOCKS + k
                     nc.tensor.transpose(eT_ps[:, k, :], e[:, sb * P : (sb + 1) * P], ident_bf[:])
                 half = eT[:, h * HALF_BLOCKS : (h + 1) * HALF_BLOCKS, :]
-                if h == 0:
-                    nc.vector.tensor_copy(half, eT_ps[:])
-                else:
-                    nc.scalar.copy(half, eT_ps[:])
+                nc.vector.tensor_copy(half, eT_ps[:])
             spread_ps = psum_out.tile([D, P], F32, name="spread_ps")
-            nc.tensor.matmul(spread_ps[:], ones_f32[:], diag[:], start=True, stop=True)
+            nc.tensor.transpose(spread_ps[:], rden[:, 0:1].to_broadcast([P, D]), ident_f32[:])
             spread = work.tile([D, P], F32, name="spread")
             nc.vector.tensor_copy(spread[:], spread_ps[:])
             o_ps = psum_out.tile([D, P], F32, name="o_ps")
@@ -131,8 +128,11 @@ def tile_scatteringawareattention_kernel(tc, x, wq, bq, offs, out):
             nc.vector.tensor_mul(o_sb[:], o_ps[:], spread[:])
             nc.sync.dma_start(out[:, jb * P : (jb + 1) * P], o_sb[:])
 
-        pending = weights_of(0)
+        scores = [scores_of(0), scores_of(1)]
+        weights = [weights_of(scores[0][0], scores[0][1])]
         for jb in range(Q_BLOCKS):
-            following = weights_of(jb + 1) if jb + 1 < Q_BLOCKS else None
-            attend(jb, pending[0], pending[1])
-            pending = following
+            if jb + 2 < Q_BLOCKS:
+                scores.append(scores_of(jb + 2))
+            if jb + 1 < Q_BLOCKS:
+                weights.append(weights_of(scores[jb + 1][0], scores[jb + 1][1]))
+            attend(jb, weights[jb][0], weights[jb][1])

@@ -29,8 +29,9 @@ def tile_scatteringawareattention_kernel(tc, x, wq, bq, offs, out):
         tc.tile_pool(name="work", bufs=3) as work,
         tc.tile_pool(name="stats", bufs=4) as stats,
         tc.psum_pool(name="psum_scores", bufs=3) as psum_scores,
-        tc.psum_pool(name="psum_flip", bufs=3) as psum_flip,
-        tc.psum_pool(name="psum_out", bufs=1) as psum_out,
+        tc.psum_pool(name="psum_flip", bufs=2) as psum_flip,
+        tc.psum_pool(name="psum_spread", bufs=1) as psum_spread,
+        tc.psum_pool(name="psum_out", bufs=2) as psum_out,
     ):
         zeros = held.tile([P, P], BF16, name="zeros")
         nc.gpsimd.memset(zeros[:], 0.0)
@@ -102,23 +103,25 @@ def tile_scatteringawareattention_kernel(tc, x, wq, bq, offs, out):
                 )
             return e, row_sum
 
-        def attend(jb, e, row_sum):
-            den = stats.tile([P, 1], F32, name="den")
-            nc.vector.tensor_add(den[:], row_sum[:, 0:1], row_sum[:, 1:2])
-            rden = stats.tile([P, 1], F32, name="rden")
-            nc.vector.reciprocal(rden[:], den[:])
+        def flipped(e):
             eT = work.tile([P, S_BLOCKS, P], BF16, name="eT")
             for h in range(S_HALVES):
                 eT_ps = psum_flip.tile([P, HALF_BLOCKS, P], BF16, name="eT_ps", tag="flip")
                 for k in range(HALF_BLOCKS):
                     sb = h * HALF_BLOCKS + k
                     nc.tensor.transpose(eT_ps[:, k, :], e[:, sb * P : (sb + 1) * P], ident_bf[:])
-                half = eT[:, h * HALF_BLOCKS : (h + 1) * HALF_BLOCKS, :]
-                nc.vector.tensor_copy(half, eT_ps[:])
-            spread_ps = psum_out.tile([D, P], F32, name="spread_ps")
+                nc.vector.tensor_copy(eT[:, h * HALF_BLOCKS : (h + 1) * HALF_BLOCKS, :], eT_ps[:])
+            return eT
+
+        def attend(jb, eT, row_sum):
+            den = stats.tile([P, 1], F32, name="den")
+            nc.vector.tensor_add(den[:], row_sum[:, 0:1], row_sum[:, 1:2])
+            rden = stats.tile([P, 1], F32, name="rden")
+            nc.vector.reciprocal(rden[:], den[:])
+            spread_ps = psum_spread.tile([D, P], F32, name="spread_ps")
             nc.tensor.transpose(spread_ps[:], rden[:, 0:1].to_broadcast([P, D]), ident_f32[:])
             spread = work.tile([D, P], F32, name="spread")
-            nc.vector.tensor_copy(spread[:], spread_ps[:])
+            nc.scalar.copy(spread[:], spread_ps[:])
             o_ps = psum_out.tile([D, P], F32, name="o_ps")
             for sb in range(S_BLOCKS):
                 nc.tensor.matmul(
@@ -128,11 +131,12 @@ def tile_scatteringawareattention_kernel(tc, x, wq, bq, offs, out):
             nc.vector.tensor_mul(o_sb[:], o_ps[:], spread[:])
             nc.sync.dma_start(out[:, jb * P : (jb + 1) * P], o_sb[:])
 
-        scores = [scores_of(0), scores_of(1)]
-        weights = [weights_of(scores[0][0], scores[0][1])]
+        waiting = None
         for jb in range(Q_BLOCKS):
-            if jb + 2 < Q_BLOCKS:
-                scores.append(scores_of(jb + 2))
-            if jb + 1 < Q_BLOCKS:
-                weights.append(weights_of(scores[jb + 1][0], scores[jb + 1][1]))
-            attend(jb, weights[jb][0], weights[jb][1])
+            negated, shift = scores_of(jb)
+            e, row_sum = weights_of(negated, shift)
+            eT = flipped(e)
+            if waiting is not None:
+                attend(jb - 1, waiting[0], waiting[1])
+            waiting = (eT, row_sum)
+        attend(Q_BLOCKS - 1, waiting[0], waiting[1])

@@ -63,7 +63,7 @@ def tile_scatteringawareattention_kernel(tc, x, wq, bq, offs, out):
         xT = held.tile([P, S_BLOCKS, D], BF16, name="xT")
         xT_ps = psum_flip.tile([P, S_BLOCKS, D], BF16, name="xT_ps", tag="flip")
         for sb in range(S_BLOCKS):
-            nc.tensor.transpose(xT_ps[:, sb, :], x_sb[:, sb * P : (sb + 1) * P], ident_bf[:])
+            nc.tensor.matmul(xT_ps[:, sb, :], x_sb[:, sb * P : (sb + 1) * P], ident_bf[:], start=True, stop=True)
         nc.vector.tensor_copy(xT[:], xT_ps[:])
 
         def scores_of(jb):
@@ -109,7 +109,7 @@ def tile_scatteringawareattention_kernel(tc, x, wq, bq, offs, out):
                 eT_ps = psum_flip.tile([P, HALF_BLOCKS, P], BF16, name="eT_ps", tag="flip")
                 for k in range(HALF_BLOCKS):
                     sb = h * HALF_BLOCKS + k
-                    nc.tensor.transpose(eT_ps[:, k, :], e[:, sb * P : (sb + 1) * P], ident_bf[:])
+                    nc.tensor.matmul(eT_ps[:, k, :], e[:, sb * P : (sb + 1) * P], ident_bf[:], start=True, stop=True)
                 nc.vector.tensor_copy(eT[:, h * HALF_BLOCKS : (h + 1) * HALF_BLOCKS, :], eT_ps[:])
             return eT
 

@@ -113,7 +113,7 @@ def tile_scatteringawareattention_kernel(tc, x, wq, bq, offs, out):
                 nc.vector.tensor_copy(eT[:, h * HALF_BLOCKS : (h + 1) * HALF_BLOCKS, :], eT_ps[:])
             return eT
 
-        def attend(jb, eT, row_sum):
+        def spread_of(row_sum):
             den = stats.tile([P, 1], F32, name="den")
             nc.vector.tensor_add(den[:], row_sum[:, 0:1], row_sum[:, 1:2])
             rden = stats.tile([P, 1], F32, name="rden")
@@ -122,6 +122,9 @@ def tile_scatteringawareattention_kernel(tc, x, wq, bq, offs, out):
             nc.tensor.transpose(spread_ps[:], rden[:, 0:1].to_broadcast([P, D]), ident_f32[:])
             spread = work.tile([D, P], F32, name="spread")
             nc.scalar.copy(spread[:], spread_ps[:])
+            return spread
+
+        def attend(jb, eT, spread):
             o_ps = psum_out.tile([D, P], F32, name="o_ps")
             for sb in range(S_BLOCKS):
                 nc.tensor.matmul(
@@ -135,8 +138,9 @@ def tile_scatteringawareattention_kernel(tc, x, wq, bq, offs, out):
         for jb in range(Q_BLOCKS):
             negated, shift = scores_of(jb)
             e, row_sum = weights_of(negated, shift)
+            spread = spread_of(row_sum)
             eT = flipped(e)
             if waiting is not None:
                 attend(jb - 1, waiting[0], waiting[1])
-            waiting = (eT, row_sum)
+            waiting = (eT, spread)
         attend(Q_BLOCKS - 1, waiting[0], waiting[1])

@@ -138,9 +138,8 @@ def tile_scatteringawareattention_kernel(tc, x, wq, bq, offs, out):
         for jb in range(Q_BLOCKS):
             negated, shift = scores_of(jb)
             e, row_sum = weights_of(negated, shift)
-            spread = spread_of(row_sum)
             eT = flipped(e)
             if waiting is not None:
                 attend(jb - 1, waiting[0], waiting[1])
-            waiting = (eT, spread)
+            waiting = (eT, spread_of(row_sum))
         attend(Q_BLOCKS - 1, waiting[0], waiting[1])

@@ -29,117 +29,123 @@ def tile_scatteringawareattention_kernel(tc, x, wq, bq, offs, out):
         tc.tile_pool(name="work", bufs=3) as work,
         tc.tile_pool(name="stats", bufs=4) as stats,
         tc.psum_pool(name="psum_scores", bufs=3) as psum_scores,
-        tc.psum_pool(name="psum_flip", bufs=2) as psum_flip,
-        tc.psum_pool(name="psum_spread", bufs=1) as psum_spread,
-        tc.psum_pool(name="psum_out", bufs=2) as psum_out,
     ):
-        zeros = held.tile([P, P], BF16, name="zeros")
-        nc.gpsimd.memset(zeros[:], 0.0)
-        warm_ps = psum_out.tile([P, P], F32, name="warm_ps", tag="o_ps")
-        for i in range(WARM_UP):
-            nc.tensor.matmul(warm_ps[:], zeros[:], zeros[:], start=True, stop=True)
+        with (
+            tc.psum_pool(name="psum_warm", bufs=1) as psum_warm,
+            tc.psum_pool(name="psum_q", bufs=Q_BLOCKS) as psum_q,
+        ):
+            zeros = held.tile([P, P], BF16, name="zeros")
+            nc.gpsimd.memset(zeros[:], 0.0)
+            warm_ps = psum_warm.tile([P, P], F32, name="warm_ps")
+            for i in range(WARM_UP):
+                nc.tensor.matmul(warm_ps[:], zeros[:], zeros[:], start=True, stop=True)
 
-        offsets = held.tile([P, N // 16], U16, name="offsets")
-        nc.sync.dma_start(offsets[:], offs)
-        x_sb = held.tile([D, S], BF16, name="x_sb")
-        nc.sync.dma_start(x_sb[:], x)
-        wq_sb = held.tile([D, D], BF16, name="wq_sb")
-        nc.scalar.dma_start(wq_sb[:], wq)
-        bq_sb = held.tile([D, 1], F32, name="bq_sb")
-        nc.scalar.dma_start(bq_sb[:], bq)
+            offsets = held.tile([P, N // 16], U16, name="offsets")
+            nc.sync.dma_start(offsets[:], offs)
+            x_sb = held.tile([D, S], BF16, name="x_sb")
+            nc.sync.dma_start(x_sb[:], x)
+            wq_sb = held.tile([D, D], BF16, name="wq_sb")
+            nc.scalar.dma_start(wq_sb[:], wq)
+            bq_sb = held.tile([D, 1], F32, name="bq_sb")
+            nc.scalar.dma_start(bq_sb[:], bq)
 
-        ident_bf = held.tile([P, P], BF16, name="ident_bf")
-        make_identity(nc, ident_bf[:])
-        ident_f32 = held.tile([P, P], F32, name="ident_f32")
-        make_identity(nc, ident_f32[:])
+            ident_bf = held.tile([P, P], BF16, name="ident_bf")
+            make_identity(nc, ident_bf[:])
+            ident_f32 = held.tile([P, P], F32, name="ident_f32")
+            make_identity(nc, ident_f32[:])
 
-        q_bf = held.tile([D, N], BF16, name="q_bf")
-        for jb in range(Q_BLOCKS):
-            q_ps = psum_scores.tile([D, P], F32, name="q_ps", tag="bank")
-            piece = offsets[:, jb * (P // 16) : (jb + 1) * (P // 16)]
-            nc.tensor.matmul(q_ps[:], wq_sb[:], x_sb[:].indirect(piece), start=True, stop=True)
-            nc.vector.tensor_scalar_add(q_bf[:, jb * P : (jb + 1) * P], q_ps[:], bq_sb[:, 0:1])
+            q_bf = held.tile([D, N], BF16, name="q_bf")
+            for jb in range(Q_BLOCKS):
+                q_ps = psum_q.tile([D, P], F32, name="q_ps")
+                piece = offsets[:, jb * (P // 16) : (jb + 1) * (P // 16)]
+                nc.tensor.matmul(q_ps[:], wq_sb[:], x_sb[:].indirect(piece), start=True, stop=True)
+                nc.vector.tensor_scalar_add(q_bf[:, jb * P : (jb + 1) * P], q_ps[:], bq_sb[:, 0:1])
 
-        xT = held.tile([P, S_BLOCKS, D], BF16, name="xT")
-        xT_ps = psum_flip.tile([P, S_BLOCKS, D], BF16, name="xT_ps", tag="flip")
-        for sb in range(S_BLOCKS):
-            nc.tensor.matmul(xT_ps[:, sb, :], x_sb[:, sb * P : (sb + 1) * P], ident_bf[:], start=True, stop=True)
-        nc.vector.tensor_copy(xT[:], xT_ps[:])
-
-        def scores_of(jb):
-            negated = work.tile([P, S], F32, name="negated")
-            lowest = stats.tile([P, S_HALVES], F32, name="lowest")
-            for h in range(S_HALVES):
-                bank = psum_scores.tile([P, BANK], F32, name="score_ps", tag="bank")
-                nc.tensor.matmul(
-                    bank[:],
-                    q_bf[:, jb * P : (jb + 1) * P],
-                    x_sb[:, h * BANK : (h + 1) * BANK],
-                    start=True,
-                    stop=True,
-                )
-                nc.vector.tensor_scalar(
-                    negated[:, h * BANK : (h + 1) * BANK],
-                    bank[:],
-                    -SCALE,
-                    None if h == 0 else lowest[:, h - 1 : h],
-                    op0=ALU.mult,
-                    op1=ALU.min,
-                    accum_out=lowest[:, h : h + 1],
-                )
-            return negated, lowest[:, S_HALVES - 1 : S_HALVES]
-
-        def weights_of(negated, shift):
-            e = work.tile([P, S], BF16, name="e")
-            row_sum = stats.tile([P, S_HALVES], F32, name="row_sum")
-            for h in range(S_HALVES):
-                nc.scalar.activation(
-                    e[:, h * BANK : (h + 1) * BANK],
-                    negated[:, h * BANK : (h + 1) * BANK],
-                    EXP,
-                    bias=shift,
-                    scale=-1.0,
-                    accum_out=row_sum[:, h : h + 1],
-                )
-            return e, row_sum
-
-        def flipped(e):
-            eT = work.tile([P, S_BLOCKS, P], BF16, name="eT")
-            for h in range(S_HALVES):
-                eT_ps = psum_flip.tile([P, HALF_BLOCKS, P], BF16, name="eT_ps", tag="flip")
-                for k in range(HALF_BLOCKS):
-                    sb = h * HALF_BLOCKS + k
-                    nc.tensor.matmul(eT_ps[:, k, :], e[:, sb * P : (sb + 1) * P], ident_bf[:], start=True, stop=True)
-                nc.vector.tensor_copy(eT[:, h * HALF_BLOCKS : (h + 1) * HALF_BLOCKS, :], eT_ps[:])
-            return eT
-
-        def spread_of(row_sum):
-            den = stats.tile([P, 1], F32, name="den")
-            nc.vector.tensor_add(den[:], row_sum[:, 0:1], row_sum[:, 1:2])
-            rden = stats.tile([P, 1], F32, name="rden")
-            nc.vector.reciprocal(rden[:], den[:])
-            spread_ps = psum_spread.tile([D, P], F32, name="spread_ps")
-            nc.tensor.transpose(spread_ps[:], rden[:, 0:1].to_broadcast([P, D]), ident_f32[:])
-            spread = work.tile([D, P], F32, name="spread")
-            nc.scalar.copy(spread[:], spread_ps[:])
-            return spread
-
-        def attend(jb, eT, spread):
-            o_ps = psum_out.tile([D, P], F32, name="o_ps")
+        with (
+            tc.psum_pool(name="psum_flip", bufs=2) as psum_flip,
+            tc.psum_pool(name="psum_spread", bufs=1) as psum_spread,
+            tc.psum_pool(name="psum_out", bufs=2) as psum_out,
+        ):
+            xT = held.tile([P, S_BLOCKS, D], BF16, name="xT")
+            xT_ps = psum_flip.tile([P, S_BLOCKS, D], BF16, name="xT_ps", tag="flip")
             for sb in range(S_BLOCKS):
-                nc.tensor.matmul(
-                    o_ps[:], xT[:, sb, :], eT[:, sb, :], start=(sb == 0), stop=(sb == S_BLOCKS - 1)
-                )
-            o_sb = work.tile([D, P], F32, name="o_sb")
-            nc.vector.tensor_mul(o_sb[:], o_ps[:], spread[:])
-            nc.sync.dma_start(out[:, jb * P : (jb + 1) * P], o_sb[:])
+                nc.tensor.matmul(xT_ps[:, sb, :], x_sb[:, sb * P : (sb + 1) * P], ident_bf[:], start=True, stop=True)
+            nc.vector.tensor_copy(xT[:], xT_ps[:])
 
-        waiting = None
-        for jb in range(Q_BLOCKS):
-            negated, shift = scores_of(jb)
-            e, row_sum = weights_of(negated, shift)
-            eT = flipped(e)
-            if waiting is not None:
-                attend(jb - 1, waiting[0], waiting[1])
-            waiting = (eT, spread_of(row_sum))
-        attend(Q_BLOCKS - 1, waiting[0], waiting[1])
+            def scores_of(jb):
+                negated = work.tile([P, S], F32, name="negated")
+                lowest = stats.tile([P, S_HALVES], F32, name="lowest")
+                for h in range(S_HALVES):
+                    bank = psum_scores.tile([P, BANK], F32, name="score_ps", tag="bank")
+                    nc.tensor.matmul(
+                        bank[:],
+                        q_bf[:, jb * P : (jb + 1) * P],
+                        x_sb[:, h * BANK : (h + 1) * BANK],
+                        start=True,
+                        stop=True,
+                    )
+                    nc.vector.tensor_scalar(
+                        negated[:, h * BANK : (h + 1) * BANK],
+                        bank[:],
+                        -SCALE,
+                        None if h == 0 else lowest[:, h - 1 : h],
+                        op0=ALU.mult,
+                        op1=ALU.min,
+                        accum_out=lowest[:, h : h + 1],
+                    )
+                return negated, lowest[:, S_HALVES - 1 : S_HALVES]
+
+            def weights_of(negated, shift):
+                e = work.tile([P, S], BF16, name="e")
+                row_sum = stats.tile([P, S_HALVES], F32, name="row_sum")
+                for h in range(S_HALVES):
+                    nc.scalar.activation(
+                        e[:, h * BANK : (h + 1) * BANK],
+                        negated[:, h * BANK : (h + 1) * BANK],
+                        EXP,
+                        bias=shift,
+                        scale=-1.0,
+                        accum_out=row_sum[:, h : h + 1],
+                    )
+                return e, row_sum
+
+            def flipped(e):
+                eT = work.tile([P, S_BLOCKS, P], BF16, name="eT")
+                for h in range(S_HALVES):
+                    eT_ps = psum_flip.tile([P, HALF_BLOCKS, P], BF16, name="eT_ps", tag="flip")
+                    for k in range(HALF_BLOCKS):
+                        sb = h * HALF_BLOCKS + k
+                        nc.tensor.matmul(eT_ps[:, k, :], e[:, sb * P : (sb + 1) * P], ident_bf[:], start=True, stop=True)
+                    nc.vector.tensor_copy(eT[:, h * HALF_BLOCKS : (h + 1) * HALF_BLOCKS, :], eT_ps[:])
+                return eT
+
+            def spread_of(row_sum):
+                den = stats.tile([P, 1], F32, name="den")
+                nc.vector.tensor_add(den[:], row_sum[:, 0:1], row_sum[:, 1:2])
+                rden = stats.tile([P, 1], F32, name="rden")
+                nc.vector.reciprocal(rden[:], den[:])
+                spread_ps = psum_spread.tile([D, P], F32, name="spread_ps")
+                nc.tensor.transpose(spread_ps[:], rden[:, 0:1].to_broadcast([P, D]), ident_f32[:])
+                spread = work.tile([D, P], F32, name="spread")
+                nc.scalar.copy(spread[:], spread_ps[:])
+                return spread
+
+            def attend(jb, eT, spread):
+                o_ps = psum_out.tile([D, P], F32, name="o_ps")
+                for sb in range(S_BLOCKS):
+                    nc.tensor.matmul(
+                        o_ps[:], xT[:, sb, :], eT[:, sb, :], start=(sb == 0), stop=(sb == S_BLOCKS - 1)
+                    )
+                o_sb = work.tile([D, P], F32, name="o_sb")
+                nc.vector.tensor_mul(o_sb[:], o_ps[:], spread[:])
+                nc.sync.dma_start(out[:, jb * P : (jb + 1) * P], o_sb[:])
+
+            waiting = None
+            for jb in range(Q_BLOCKS):
+                negated, shift = scores_of(jb)
+                e, row_sum = weights_of(negated, shift)
+                eT = flipped(e)
+                if waiting is not None:
+                    attend(jb - 1, waiting[0], waiting[1])
+                waiting = (eT, spread_of(row_sum))
+            attend(Q_BLOCKS - 1, waiting[0], waiting[1])

@@ -1,10 +1,10 @@
 import math
 
 import concourse.mybir as mybir
-from concourse.masks import make_identity
 
 BF16, F32, U16 = mybir.dt.bfloat16, mybir.dt.float32, mybir.dt.uint16
 EXP = mybir.ActivationFunctionType.Exp
+IDENTITY = mybir.ActivationFunctionType.Identity
 ALU = mybir.AluOpType
 
 P = 128
@@ -16,7 +16,8 @@ S_BLOCKS = S // P
 S_HALVES = S // BANK
 HALF_BLOCKS = S_BLOCKS // S_HALVES
 Q_BLOCKS = N // P
-WARM_UP = 16
+FLIP_BANKS = 2
+WARM_UP = 14
 SCALE = 1.0 / math.sqrt(D)
 
 FLOPS = 2 * D * N * (D + S + S)
@@ -26,126 +27,139 @@ def tile_scatteringawareattention_kernel(tc, x, wq, bq, offs, out):
     nc = tc.nc
     with (
         tc.tile_pool(name="held", bufs=1) as held,
-        tc.tile_pool(name="work", bufs=3) as work,
-        tc.tile_pool(name="stats", bufs=4) as stats,
+        tc.tile_pool(name="work", bufs=Q_BLOCKS) as work,
+        tc.tile_pool(name="stats", bufs=Q_BLOCKS) as stats,
         tc.psum_pool(name="psum_scores", bufs=3) as psum_scores,
+        tc.psum_pool(name="psum_flip", bufs=FLIP_BANKS) as psum_flip,
+        tc.psum_pool(name="psum_spread", bufs=1) as psum_spread,
+        tc.psum_pool(name="psum_out", bufs=2) as psum_out,
     ):
-        with (
-            tc.psum_pool(name="psum_warm", bufs=1) as psum_warm,
-            tc.psum_pool(name="psum_q", bufs=Q_BLOCKS) as psum_q,
-        ):
-            zeros = held.tile([P, P], BF16, name="zeros")
-            nc.gpsimd.memset(zeros[:], 0.0)
-            warm_ps = psum_warm.tile([P, P], F32, name="warm_ps")
-            for i in range(WARM_UP):
-                nc.tensor.matmul(warm_ps[:], zeros[:], zeros[:], start=True, stop=True)
+        share = held.tile([P, P], BF16, name="share")
+        nc.vector.memset(share[:], 1.0 / P)
+        early_ps = psum_spread.tile([P, 2, P], F32, name="early_ps", tag="spread")
+        for i in range(WARM_UP):
+            nc.tensor.matmul(early_ps[:, 0, :], share[:], share[:], start=True, stop=True)
+        ones = held.tile([P, P], F32, name="ones")
+        nc.vector.memset(ones[:], 1.0)
+        count = held.tile([P, P], F32, name="count")
+        nc.vector.tensor_tensor_scan(count[:], ones[:], ones[:], 0.0, op0=ALU.mult, op1=ALU.add)
+        count_bf = held.tile([P, P], BF16, name="count_bf")
+        nc.vector.tensor_copy(count_bf[:], count[:])
+        nc.tensor.matmul(early_ps[:, 1, :], count_bf[:], share[:], start=True, stop=True)
+        ident_bf = held.tile([P, P], BF16, name="ident_bf")
+        nc.vector.tensor_tensor(ident_bf[:], early_ps[:, 1, :], count[:], ALU.is_equal)
+        ident_f32 = held.tile([P, P], F32, name="ident_f32")
+        nc.vector.tensor_copy(ident_f32[:], ident_bf[:])
 
-            offsets = held.tile([P, N // 16], U16, name="offsets")
-            nc.sync.dma_start(offsets[:], offs)
-            x_sb = held.tile([D, S], BF16, name="x_sb")
-            nc.sync.dma_start(x_sb[:], x)
-            wq_sb = held.tile([D, D], BF16, name="wq_sb")
-            nc.scalar.dma_start(wq_sb[:], wq)
-            bq_sb = held.tile([D, 1], F32, name="bq_sb")
-            nc.scalar.dma_start(bq_sb[:], bq)
+        offsets = held.tile([P, N // 16], U16, name="offsets")
+        nc.sync.dma_start(offsets[:], offs)
+        x_sb = held.tile([D, S], BF16, name="x_sb")
+        nc.sync.dma_start(x_sb[:], x)
+        wq_sb = held.tile([D, D], BF16, name="wq_sb")
+        nc.scalar.dma_start(wq_sb[:], wq)
+        bq_sb = held.tile([D, 1], F32, name="bq_sb")
+        nc.scalar.dma_start(bq_sb[:], bq)
 
-            ident_bf = held.tile([P, P], BF16, name="ident_bf")
-            make_identity(nc, ident_bf[:])
-            ident_f32 = held.tile([P, P], F32, name="ident_f32")
-            make_identity(nc, ident_f32[:])
+        first_exp = held.tile([P, 1], F32, name="first_exp")
+        nc.scalar.activation(first_exp[:], share[:, 0:1], EXP)
 
-            q_bf = held.tile([D, N], BF16, name="q_bf")
-            for jb in range(Q_BLOCKS):
-                q_ps = psum_q.tile([D, P], F32, name="q_ps")
-                piece = offsets[:, jb * (P // 16) : (jb + 1) * (P // 16)]
-                nc.tensor.matmul(q_ps[:], wq_sb[:], x_sb[:].indirect(piece), start=True, stop=True)
-                nc.vector.tensor_scalar_add(q_bf[:, jb * P : (jb + 1) * P], q_ps[:], bq_sb[:, 0:1])
+        q_bf = held.tile([D, N], BF16, name="q_bf")
+        for jb in range(Q_BLOCKS):
+            if jb < FLIP_BANKS:
+                q_ps = psum_flip.tile([D, P], F32, name="q_ps", tag="flip")
+            else:
+                q_ps = psum_out.tile([D, P], F32, name="q_ps", tag="out")
+            piece = offsets[:, jb * (P // 16) : (jb + 1) * (P // 16)]
+            nc.tensor.matmul(q_ps[:], wq_sb[:], x_sb[:].indirect(piece), start=True, stop=True)
+            nc.vector.tensor_scalar_add(q_bf[:, jb * P : (jb + 1) * P], q_ps[:], bq_sb[:, 0:1])
 
-        with (
-            tc.psum_pool(name="psum_flip", bufs=2) as psum_flip,
-            tc.psum_pool(name="psum_spread", bufs=1) as psum_spread,
-            tc.psum_pool(name="psum_out", bufs=2) as psum_out,
-        ):
-            xT = held.tile([P, S_BLOCKS, D], BF16, name="xT")
-            xT_ps = psum_flip.tile([P, S_BLOCKS, D], BF16, name="xT_ps", tag="flip")
+        def scores_of(jb):
+            negated = work.tile([P, S], F32, name="negated")
+            lowest = stats.tile([P, S_HALVES], F32, name="lowest")
+            for h in range(S_HALVES):
+                bank = psum_scores.tile([P, BANK], F32, name="score_ps", tag="bank")
+                nc.tensor.matmul(
+                    bank[:],
+                    q_bf[:, jb * P : (jb + 1) * P],
+                    x_sb[:, h * BANK : (h + 1) * BANK],
+                    start=True,
+                    stop=True,
+                )
+                nc.vector.tensor_scalar(
+                    negated[:, h * BANK : (h + 1) * BANK],
+                    bank[:],
+                    -SCALE,
+                    None,
+                    op0=ALU.mult,
+                    op1=ALU.min,
+                    accum_out=lowest[:, h : h + 1],
+                )
+            shift = stats.tile([P, 1], F32, name="shift")
+            nc.vector.tensor_tensor(shift[:], lowest[:, 0:1], lowest[:, 1:2], ALU.min)
+            return negated, shift
+
+        def weights_of(negated, shift):
+            e = work.tile([P, S], BF16, name="e")
+            row_sum = stats.tile([P, S_HALVES], F32, name="row_sum")
+            for h in range(S_HALVES):
+                nc.scalar.activation(
+                    e[:, h * BANK : (h + 1) * BANK],
+                    negated[:, h * BANK : (h + 1) * BANK],
+                    EXP,
+                    bias=shift[:],
+                    scale=-1.0,
+                    accum_out=row_sum[:, h : h + 1],
+                )
+            return e, row_sum
+
+        def flipped(jb, e):
+            eT = work.tile([P, S_BLOCKS, P], BF16, name="eT")
+            step = S_BLOCKS if jb + 1 < Q_BLOCKS else HALF_BLOCKS
+            for first in range(0, S_BLOCKS, step):
+                eT_ps = psum_flip.tile([P, step, P], BF16, name="eT_ps", tag="flip")
+                for k in range(step):
+                    sb = first + k
+                    nc.tensor.matmul(eT_ps[:, k, :], e[:, sb * P : (sb + 1) * P], ident_bf[:], start=True, stop=True)
+                nc.vector.tensor_copy(eT[:, first : first + step, :], eT_ps[:])
+            return eT
+
+        def spread_of(row_sum):
+            den = stats.tile([P, 1], F32, name="den")
+            nc.scalar.activation(den[:], row_sum[:, 1:2], IDENTITY, bias=row_sum[:, 0:1])
+            rden = stats.tile([P, 1], F32, name="rden")
+            nc.vector.reciprocal(rden[:], den[:])
+            spread_ps = psum_spread.tile([D, P], F32, name="spread_ps", tag="spread")
+            nc.tensor.transpose(spread_ps[:], rden[:, 0:1].to_broadcast([P, D]), ident_f32[:])
+            spread = work.tile([D, P], F32, name="spread")
+            nc.scalar.copy(spread[:], spread_ps[:])
+            return spread
+
+        def attend(jb, eT, spread):
+            o_ps = psum_out.tile([D, P], F32, name="o_ps", tag="out")
             for sb in range(S_BLOCKS):
-                nc.tensor.matmul(xT_ps[:, sb, :], x_sb[:, sb * P : (sb + 1) * P], ident_bf[:], start=True, stop=True)
-            nc.vector.tensor_copy(xT[:], xT_ps[:])
+                nc.tensor.matmul(o_ps[:], xT[:, sb, :], eT[:, sb, :], start=(sb == 0), stop=(sb == S_BLOCKS - 1))
+            o_sb = work.tile([D, P], F32, name="o_sb")
+            nc.vector.tensor_mul(o_sb[:], o_ps[:], spread[:])
+            nc.sync.dma_start(out[:, jb * P : (jb + 1) * P], o_sb[:])
 
-            def scores_of(jb):
-                negated = work.tile([P, S], F32, name="negated")
-                lowest = stats.tile([P, S_HALVES], F32, name="lowest")
-                for h in range(S_HALVES):
-                    bank = psum_scores.tile([P, BANK], F32, name="score_ps", tag="bank")
-                    nc.tensor.matmul(
-                        bank[:],
-                        q_bf[:, jb * P : (jb + 1) * P],
-                        x_sb[:, h * BANK : (h + 1) * BANK],
-                        start=True,
-                        stop=True,
-                    )
-                    nc.vector.tensor_scalar(
-                        negated[:, h * BANK : (h + 1) * BANK],
-                        bank[:],
-                        -SCALE,
-                        None if h == 0 else lowest[:, h - 1 : h],
-                        op0=ALU.mult,
-                        op1=ALU.min,
-                        accum_out=lowest[:, h : h + 1],
-                    )
-                return negated, lowest[:, S_HALVES - 1 : S_HALVES]
+        scores = [scores_of(0)]
 
-            def weights_of(negated, shift):
-                e = work.tile([P, S], BF16, name="e")
-                row_sum = stats.tile([P, S_HALVES], F32, name="row_sum")
-                for h in range(S_HALVES):
-                    nc.scalar.activation(
-                        e[:, h * BANK : (h + 1) * BANK],
-                        negated[:, h * BANK : (h + 1) * BANK],
-                        EXP,
-                        bias=shift,
-                        scale=-1.0,
-                        accum_out=row_sum[:, h : h + 1],
-                    )
-                return e, row_sum
+        xT = held.tile([P, S_BLOCKS, D], BF16, name="xT")
+        for h in range(S_HALVES):
+            xT_ps = psum_flip.tile([P, HALF_BLOCKS, D], BF16, name="xT_ps", tag="flip")
+            for k in range(HALF_BLOCKS):
+                sb = h * HALF_BLOCKS + k
+                nc.tensor.matmul(xT_ps[:, k, :], x_sb[:, sb * P : (sb + 1) * P], ident_bf[:], start=True, stop=True)
+            nc.scalar.copy(xT[:, h * HALF_BLOCKS : (h + 1) * HALF_BLOCKS, :], xT_ps[:])
 
-            def flipped(e):
-                eT = work.tile([P, S_BLOCKS, P], BF16, name="eT")
-                for h in range(S_HALVES):
-                    eT_ps = psum_flip.tile([P, HALF_BLOCKS, P], BF16, name="eT_ps", tag="flip")
-                    for k in range(HALF_BLOCKS):
-                        sb = h * HALF_BLOCKS + k
-                        nc.tensor.matmul(eT_ps[:, k, :], e[:, sb * P : (sb + 1) * P], ident_bf[:], start=True, stop=True)
-                    nc.vector.tensor_copy(eT[:, h * HALF_BLOCKS : (h + 1) * HALF_BLOCKS, :], eT_ps[:])
-                return eT
-
-            def spread_of(row_sum):
-                den = stats.tile([P, 1], F32, name="den")
-                nc.vector.tensor_add(den[:], row_sum[:, 0:1], row_sum[:, 1:2])
-                rden = stats.tile([P, 1], F32, name="rden")
-                nc.vector.reciprocal(rden[:], den[:])
-                spread_ps = psum_spread.tile([D, P], F32, name="spread_ps")
-                nc.tensor.transpose(spread_ps[:], rden[:, 0:1].to_broadcast([P, D]), ident_f32[:])
-                spread = work.tile([D, P], F32, name="spread")
-                nc.scalar.copy(spread[:], spread_ps[:])
-                return spread
-
-            def attend(jb, eT, spread):
-                o_ps = psum_out.tile([D, P], F32, name="o_ps")
-                for sb in range(S_BLOCKS):
-                    nc.tensor.matmul(
-                        o_ps[:], xT[:, sb, :], eT[:, sb, :], start=(sb == 0), stop=(sb == S_BLOCKS - 1)
-                    )
-                o_sb = work.tile([D, P], F32, name="o_sb")
-                nc.vector.tensor_mul(o_sb[:], o_ps[:], spread[:])
-                nc.sync.dma_start(out[:, jb * P : (jb + 1) * P], o_sb[:])
-
-            waiting = None
-            for jb in range(Q_BLOCKS):
-                negated, shift = scores_of(jb)
-                e, row_sum = weights_of(negated, shift)
-                eT = flipped(e)
-                if waiting is not None:
-                    attend(jb - 1, waiting[0], waiting[1])
-                waiting = (eT, spread_of(row_sum))
-            attend(Q_BLOCKS - 1, waiting[0], waiting[1])
+        scores.append(scores_of(1))
+        waiting = None
+        for jb in range(Q_BLOCKS):
+            if jb + 2 < Q_BLOCKS:
+                scores.append(scores_of(jb + 2))
+            e, row_sum = weights_of(scores[jb][0], scores[jb][1])
+            eT = flipped(jb, e)
+            if waiting is not None:
+                attend(jb - 1, waiting[0], waiting[1])
+            waiting = (eT, spread_of(row_sum))
+        attend(Q_BLOCKS - 1, waiting[0], waiting[1])

@@ -16,7 +16,8 @@ S_BLOCKS = S // P
 S_HALVES = S // BANK
 HALF_BLOCKS = S_BLOCKS // S_HALVES
 Q_BLOCKS = N // P
-FLIP_BANKS = 2
+FLIP_BANKS = 3
+SCORES_AHEAD = 3
 WARM_UP = 14
 SCALE = 1.0 / math.sqrt(D)
 
@@ -31,12 +32,11 @@ def tile_scatteringawareattention_kernel(tc, x, wq, bq, offs, out):
         tc.tile_pool(name="stats", bufs=Q_BLOCKS) as stats,
         tc.psum_pool(name="psum_scores", bufs=3) as psum_scores,
         tc.psum_pool(name="psum_flip", bufs=FLIP_BANKS) as psum_flip,
-        tc.psum_pool(name="psum_spread", bufs=1) as psum_spread,
         tc.psum_pool(name="psum_out", bufs=2) as psum_out,
     ):
         share = held.tile([P, P], BF16, name="share")
         nc.vector.memset(share[:], 1.0 / P)
-        early_ps = psum_spread.tile([P, 2, P], F32, name="early_ps", tag="spread")
+        early_ps = psum_out.tile([P, 2, P], F32, name="early_ps", tag="out")
         for i in range(WARM_UP):
             nc.tensor.matmul(early_ps[:, 0, :], share[:], share[:], start=True, stop=True)
         ones = held.tile([P, P], F32, name="ones")
@@ -76,6 +76,7 @@ def tile_scatteringawareattention_kernel(tc, x, wq, bq, offs, out):
         def scores_of(jb):
             negated = work.tile([P, S], F32, name="negated")
             lowest = stats.tile([P, S_HALVES], F32, name="lowest")
+            chained = jb == Q_BLOCKS - 1
             for h in range(S_HALVES):
                 bank = psum_scores.tile([P, BANK], F32, name="score_ps", tag="bank")
                 nc.tensor.matmul(
@@ -89,32 +90,43 @@ def tile_scatteringawareattention_kernel(tc, x, wq, bq, offs, out):
                     negated[:, h * BANK : (h + 1) * BANK],
                     bank[:],
                     -SCALE,
-                    None,
+                    lowest[:, 0:1] if chained and h > 0 else None,
                     op0=ALU.mult,
                     op1=ALU.min,
                     accum_out=lowest[:, h : h + 1],
                 )
+            if chained:
+                return negated, lowest[:, 1:2]
             shift = stats.tile([P, 1], F32, name="shift")
             nc.vector.tensor_tensor(shift[:], lowest[:, 0:1], lowest[:, 1:2], ALU.min)
-            return negated, shift
+            return negated, shift[:]
 
-        def weights_of(negated, shift):
+        def pieces_of(jb):
+            return 1 if jb + 1 < Q_BLOCKS else S_HALVES
+
+        def weights_of(jb, negated, shift):
             e = work.tile([P, S], BF16, name="e")
-            row_sum = stats.tile([P, S_HALVES], F32, name="row_sum")
-            for h in range(S_HALVES):
+            pieces = pieces_of(jb)
+            width = S // pieces
+            row_sum = stats.tile([P, pieces], F32, name="row_sum")
+            for i in range(pieces):
                 nc.scalar.activation(
-                    e[:, h * BANK : (h + 1) * BANK],
-                    negated[:, h * BANK : (h + 1) * BANK],
+                    e[:, i * width : (i + 1) * width],
+                    negated[:, i * width : (i + 1) * width],
                     EXP,
-                    bias=shift[:],
+                    bias=shift,
                     scale=-1.0,
-                    accum_out=row_sum[:, h : h + 1],
+                    accum_out=row_sum[:, i : i + 1],
                 )
-            return e, row_sum
+            if pieces == 1:
+                return e, row_sum
+            den = stats.tile([P, 1], F32, name="den")
+            nc.scalar.activation(den[:], row_sum[:, 1:2], IDENTITY, bias=row_sum[:, 0:1])
+            return e, den
 
         def flipped(jb, e):
             eT = work.tile([P, S_BLOCKS, P], BF16, name="eT")
-            step = S_BLOCKS if jb + 1 < Q_BLOCKS else HALF_BLOCKS
+            step = S_BLOCKS // pieces_of(jb)
             for first in range(0, S_BLOCKS, step):
                 eT_ps = psum_flip.tile([P, step, P], BF16, name="eT_ps", tag="flip")
                 for k in range(step):
@@ -123,18 +135,17 @@ def tile_scatteringawareattention_kernel(tc, x, wq, bq, offs, out):
                 nc.vector.tensor_copy(eT[:, first : first + step, :], eT_ps[:])
             return eT
 
-        def spread_of(row_sum):
-            den = stats.tile([P, 1], F32, name="den")
-            nc.scalar.activation(den[:], row_sum[:, 1:2], IDENTITY, bias=row_sum[:, 0:1])
+        def spread_of(den):
             rden = stats.tile([P, 1], F32, name="rden")
             nc.vector.reciprocal(rden[:], den[:])
-            spread_ps = psum_spread.tile([D, P], F32, name="spread_ps", tag="spread")
+            spread_ps = psum_scores.tile([D, P], F32, name="spread_ps", tag="bank")
             nc.tensor.transpose(spread_ps[:], rden[:, 0:1].to_broadcast([P, D]), ident_f32[:])
             spread = work.tile([D, P], F32, name="spread")
             nc.scalar.copy(spread[:], spread_ps[:])
             return spread
 
-        def attend(jb, eT, spread):
+        def attend(jb, eT, den):
+            spread = spread_of(den)
             o_ps = psum_out.tile([D, P], F32, name="o_ps", tag="out")
             for sb in range(S_BLOCKS):
                 nc.tensor.matmul(o_ps[:], xT[:, sb, :], eT[:, sb, :], start=(sb == 0), stop=(sb == S_BLOCKS - 1))
@@ -152,14 +163,13 @@ def tile_scatteringawareattention_kernel(tc, x, wq, bq, offs, out):
                 nc.tensor.matmul(xT_ps[:, k, :], x_sb[:, sb * P : (sb + 1) * P], ident_bf[:], start=True, stop=True)
             nc.scalar.copy(xT[:, h * HALF_BLOCKS : (h + 1) * HALF_BLOCKS, :], xT_ps[:])
 
-        scores.append(scores_of(1))
-        waiting = None
+        scores.extend(scores_of(jb) for jb in range(1, SCORES_AHEAD))
+        weights = []
         for jb in range(Q_BLOCKS):
-            if jb + 2 < Q_BLOCKS:
-                scores.append(scores_of(jb + 2))
-            e, row_sum = weights_of(scores[jb][0], scores[jb][1])
-            eT = flipped(jb, e)
-            if waiting is not None:
-                attend(jb - 1, waiting[0], waiting[1])
-            waiting = (eT, spread_of(row_sum))
-        attend(Q_BLOCKS - 1, waiting[0], waiting[1])
+            e, den = weights_of(jb, scores[jb][0], scores[jb][1])
+            weights.append((flipped(jb, e), den))
+            if jb + SCORES_AHEAD < Q_BLOCKS:
+                scores.append(scores_of(jb + SCORES_AHEAD))
+            if jb > 0:
+                attend(jb - 1, weights[jb - 1][0], weights[jb - 1][1])
+        attend(Q_BLOCKS - 1, weights[-1][0], weights[-1][1])

@@ -102,7 +102,7 @@ def tile_scatteringawareattention_kernel(tc, x, wq, bq, offs, out):
             return negated, shift[:]
 
         def pieces_of(jb):
-            return 1 if jb + 1 < Q_BLOCKS else S_HALVES
+            return S_HALVES if jb in (0, Q_BLOCKS - 1) else 1
 
         def weights_of(jb, negated, shift):
             e = work.tile([P, S], BF16, name="e")

@@ -52,9 +52,9 @@ def tile_scatteringawareattention_kernel(tc, x, wq, bq, offs, out):
         nc.vector.tensor_copy(ident_f32[:], ident_bf[:])
 
         offsets = held.tile([P, N // 16], U16, name="offsets")
-        nc.sync.dma_start(offsets[:], offs)
         x_sb = held.tile([D, S], BF16, name="x_sb")
         nc.sync.dma_start(x_sb[:], x)
+        nc.sync.dma_start(offsets[:], offs)
         wq_sb = held.tile([D, D], BF16, name="wq_sb")
         nc.scalar.dma_start(wq_sb[:], wq)
         bq_sb = held.tile([D, 1], F32, name="bq_sb")

import math

import concourse.mybir as mybir

BF16, F32, U16 = mybir.dt.bfloat16, mybir.dt.float32, mybir.dt.uint16
EXP = mybir.ActivationFunctionType.Exp
IDENTITY = mybir.ActivationFunctionType.Identity
ALU = mybir.AluOpType

P = 128
D = 128
S = 1024
N = 512
BANK = 512
S_BLOCKS = S // P
S_HALVES = S // BANK
HALF_BLOCKS = S_BLOCKS // S_HALVES
Q_BLOCKS = N // P
FLIP_BANKS = 3
SCORES_AHEAD = 3
WARM_UP = 14
SCALE = 1.0 / math.sqrt(D)

FLOPS = 2 * D * N * (D + S + S)


def tile_scatteringawareattention_kernel(tc, x, wq, bq, offs, out):
    nc = tc.nc
    with (
        tc.tile_pool(name="held", bufs=1) as held,
        tc.tile_pool(name="work", bufs=Q_BLOCKS) as work,
        tc.tile_pool(name="stats", bufs=Q_BLOCKS) as stats,
        tc.psum_pool(name="psum_scores", bufs=3) as psum_scores,
        tc.psum_pool(name="psum_flip", bufs=FLIP_BANKS) as psum_flip,
        tc.psum_pool(name="psum_out", bufs=2) as psum_out,
    ):
        share = held.tile([P, P], BF16, name="share")
        nc.vector.memset(share[:], 1.0 / P)
        early_ps = psum_out.tile([P, 2, P], F32, name="early_ps", tag="out")
        for i in range(WARM_UP):
            nc.tensor.matmul(early_ps[:, 0, :], share[:], share[:], start=True, stop=True)
        ones = held.tile([P, P], F32, name="ones")
        nc.vector.memset(ones[:], 1.0)
        count = held.tile([P, P], F32, name="count")
        nc.vector.tensor_tensor_scan(count[:], ones[:], ones[:], 0.0, op0=ALU.mult, op1=ALU.add)
        count_bf = held.tile([P, P], BF16, name="count_bf")
        nc.vector.tensor_copy(count_bf[:], count[:])
        nc.tensor.matmul(early_ps[:, 1, :], count_bf[:], share[:], start=True, stop=True)
        ident_bf = held.tile([P, P], BF16, name="ident_bf")
        nc.vector.tensor_tensor(ident_bf[:], early_ps[:, 1, :], count[:], ALU.is_equal)
        ident_f32 = held.tile([P, P], F32, name="ident_f32")
        nc.vector.tensor_copy(ident_f32[:], ident_bf[:])

        offsets = held.tile([P, N // 16], U16, name="offsets")
        x_sb = held.tile([D, S], BF16, name="x_sb")
        nc.sync.dma_start(x_sb[:], x)
        nc.sync.dma_start(offsets[:], offs)
        wq_sb = held.tile([D, D], BF16, name="wq_sb")
        nc.scalar.dma_start(wq_sb[:], wq)
        bq_sb = held.tile([D, 1], F32, name="bq_sb")
        nc.scalar.dma_start(bq_sb[:], bq)

        first_exp = held.tile([P, 1], F32, name="first_exp")
        nc.scalar.activation(first_exp[:], share[:, 0:1], EXP)

        q_bf = held.tile([D, N], BF16, name="q_bf")
        for jb in range(Q_BLOCKS):
            if jb < FLIP_BANKS:
                q_ps = psum_flip.tile([D, P], F32, name="q_ps", tag="flip")
            else:
                q_ps = psum_out.tile([D, P], F32, name="q_ps", tag="out")
            piece = offsets[:, jb * (P // 16) : (jb + 1) * (P // 16)]
            nc.tensor.matmul(q_ps[:], wq_sb[:], x_sb[:].indirect(piece), start=True, stop=True)
            nc.vector.tensor_scalar_add(q_bf[:, jb * P : (jb + 1) * P], q_ps[:], bq_sb[:, 0:1])

        def scores_of(jb):
            negated = work.tile([P, S], F32, name="negated")
            lowest = stats.tile([P, S_HALVES], F32, name="lowest")
            chained = jb == Q_BLOCKS - 1
            for h in range(S_HALVES):
                bank = psum_scores.tile([P, BANK], F32, name="score_ps", tag="bank")
                nc.tensor.matmul(
                    bank[:],
                    q_bf[:, jb * P : (jb + 1) * P],
                    x_sb[:, h * BANK : (h + 1) * BANK],
                    start=True,
                    stop=True,
                )
                nc.vector.tensor_scalar(
                    negated[:, h * BANK : (h + 1) * BANK],
                    bank[:],
                    -SCALE,
                    lowest[:, 0:1] if chained and h > 0 else None,
                    op0=ALU.mult,
                    op1=ALU.min,
                    accum_out=lowest[:, h : h + 1],
                )
            if chained:
                return negated, lowest[:, 1:2]
            shift = stats.tile([P, 1], F32, name="shift")
            nc.vector.tensor_tensor(shift[:], lowest[:, 0:1], lowest[:, 1:2], ALU.min)
            return negated, shift[:]

        def pieces_of(jb):
            return S_HALVES if jb in (0, Q_BLOCKS - 1) else 1

        def weights_of(jb, negated, shift):
            e = work.tile([P, S], BF16, name="e")
            pieces = pieces_of(jb)
            width = S // pieces
            row_sum = stats.tile([P, pieces], F32, name="row_sum")
            for i in range(pieces):
                nc.scalar.activation(
                    e[:, i * width : (i + 1) * width],
                    negated[:, i * width : (i + 1) * width],
                    EXP,
                    bias=shift,
                    scale=-1.0,
                    accum_out=row_sum[:, i : i + 1],
                )
            if pieces == 1:
                return e, row_sum
            den = stats.tile([P, 1], F32, name="den")
            nc.scalar.activation(den[:], row_sum[:, 1:2], IDENTITY, bias=row_sum[:, 0:1])
            return e, den

        def flipped(jb, e):
            eT = work.tile([P, S_BLOCKS, P], BF16, name="eT")
            step = S_BLOCKS // pieces_of(jb)
            for first in range(0, S_BLOCKS, step):
                eT_ps = psum_flip.tile([P, step, P], BF16, name="eT_ps", tag="flip")
                for k in range(step):
                    sb = first + k
                    nc.tensor.matmul(eT_ps[:, k, :], e[:, sb * P : (sb + 1) * P], ident_bf[:], start=True, stop=True)
                nc.vector.tensor_copy(eT[:, first : first + step, :], eT_ps[:])
            return eT

        def spread_of(den):
            rden = stats.tile([P, 1], F32, name="rden")
            nc.vector.reciprocal(rden[:], den[:])
            spread_ps = psum_scores.tile([D, P], F32, name="spread_ps", tag="bank")
            nc.tensor.transpose(spread_ps[:], rden[:, 0:1].to_broadcast([P, D]), ident_f32[:])
            spread = work.tile([D, P], F32, name="spread")
            nc.scalar.copy(spread[:], spread_ps[:])
            return spread

        def attend(jb, eT, den):
            spread = spread_of(den)
            o_ps = psum_out.tile([D, P], F32, name="o_ps", tag="out")
            for sb in range(S_BLOCKS):
                nc.tensor.matmul(o_ps[:], xT[:, sb, :], eT[:, sb, :], start=(sb == 0), stop=(sb == S_BLOCKS - 1))
            o_sb = work.tile([D, P], F32, name="o_sb")
            nc.vector.tensor_mul(o_sb[:], o_ps[:], spread[:])
            nc.sync.dma_start(out[:, jb * P : (jb + 1) * P], o_sb[:])

        scores = [scores_of(0)]

        xT = held.tile([P, S_BLOCKS, D], BF16, name="xT")
        for h in range(S_HALVES):
            xT_ps = psum_flip.tile([P, HALF_BLOCKS, D], BF16, name="xT_ps", tag="flip")
            for k in range(HALF_BLOCKS):
                sb = h * HALF_BLOCKS + k
                nc.tensor.matmul(xT_ps[:, k, :], x_sb[:, sb * P : (sb + 1) * P], ident_bf[:], start=True, stop=True)
            nc.scalar.copy(xT[:, h * HALF_BLOCKS : (h + 1) * HALF_BLOCKS, :], xT_ps[:])

        scores.extend(scores_of(jb) for jb in range(1, SCORES_AHEAD))
        weights = []
        for jb in range(Q_BLOCKS):
            e, den = weights_of(jb, scores[jb][0], scores[jb][1])
            weights.append((flipped(jb, e), den))
            if jb + SCORES_AHEAD < Q_BLOCKS:
                scores.append(scores_of(jb + SCORES_AHEAD))
            if jb > 0:
                attend(jb - 1, weights[jb - 1][0], weights[jb - 1][1])
        attend(Q_BLOCKS - 1, weights[-1][0], weights[-1][1])
